import numpy as np
import ml_dtypes


def mxq(x, axis, fmt="e4m3"):
    dtype, down = {"e4m3": (ml_dtypes.float8_e4m3fn, 7), "e5m2": (ml_dtypes.float8_e5m2, 14)}[fmt]
    v = np.moveaxis(np.asarray(x, np.float32).astype(ml_dtypes.bfloat16).astype(np.float64), axis, -1)
    blocks = v.reshape(v.shape[:-1] + (-1, 32))
    amax = np.abs(blocks).max(-1, keepdims=True)
    byte = np.maximum(np.where(amax > 0, np.frexp(amax)[1] - 1 + 127, 0) - down, 1)
    scale = np.exp2(byte - 127.0)
    codes = (blocks / scale).astype(np.float32).astype(dtype).astype(np.float64)
    return np.moveaxis((codes * scale).reshape(v.shape), -1, axis)


WIDE = False


def mx_kscale(k):
    if not WIDE:
        return np.ones(k)
    levels = np.array([10, -10, 5, -5, 0])
    a = np.random.permutation(np.resize(levels, k // 512 * 4)).reshape(k // 512, 4)
    idx = np.arange(k)
    return np.exp2(a[idx // 512, idx % 128 // 32])


BF16 = ml_dtypes.bfloat16


def bf(x):
    return np.asarray(x, np.float32).astype(BF16)


def f64(x):
    return np.asarray(x).astype(np.float64)


B, CL, CH, CK, CV, CO, H, W = 2, 1024, 512, 256, 512, 512, 48, 72
N = H * W
CF = CO + CH
EPS = 1e-5


def setup_inputs():
    s = mx_kscale(CV)
    t = mx_kscale(CF)
    tc, th = t[:CO], t[CO:]
    return {"context": bf(np.random.standard_normal((B, CV, H, W)) * 0.4 * s[None, :, None, None]),
            "high_feats": bf(np.random.standard_normal((B, CH, H, W)) * th[None, :, None, None]),
            "ww": bf(np.random.standard_normal((CO, CV)) * 2.0 / np.sqrt(CV) / s[None, :] * tc[:, None]),
            "bw": bf(np.random.standard_normal(CO) * 0.3 * tc),
            "wf": bf(np.random.standard_normal((CO, CF)) / np.sqrt(CF) / t[None, :]),
            "bfuse": bf(np.random.standard_normal(CO) * 0.3),
            "gf": bf(np.random.uniform(0.5, 1.5, CO)),
            "bef": bf(np.random.standard_normal(CO) * 0.3),
            "mf": bf(np.random.standard_normal(CO) * 0.3),
            "vf": bf(np.random.uniform(0.5, 1.5, CO))}


def reference(context, high_feats, ww, bw, wf, bfuse, gf, bef, mf, vf):
    ctx = f64(context).reshape(B, CV, N)
    hi = f64(high_feats).reshape(B, CH, N)
    c = (mxq(f64(ww), 1, "e4m3") @ mxq(ctx, 1, "e4m3")) + f64(bw)[None, :, None]
    fused = np.concatenate([c, hi], axis=1)
    y = (mxq(f64(wf), 1, "e4m3") @ mxq(fused, 1, "e4m3")) + f64(bfuse)[None, :, None]
    sc = f64(gf) / np.sqrt(f64(vf) + EPS)
    out = (y - f64(mf)[None, :, None]) * sc[None, :, None] + f64(bef)[None, :, None]
    return out.reshape(B, CO, H, W)

@@ -1,0 +1,326 @@
+from contextlib import ExitStack
+
+import concourse.mybir as mybir
+from concourse.masks import make_identity
+
+F32 = mybir.dt.float32
+BF16 = mybir.dt.bfloat16
+U32 = mybir.dt.uint32
+U8 = mybir.dt.uint8
+FP8X4 = mybir.dt.float8_e4m3fn_x4
+IDENTITY = mybir.ActivationFunctionType.Identity
+MULT = mybir.AluOpType.mult
+ADD = mybir.AluOpType.add
+
+P = 128
+PACK = 4
+K_PASS = P * PACK
+
+BATCH, PIXELS = 2, 48 * 72
+CV, CH, CO = 512, 512, 512
+COLS = BATCH * PIXELS
+CHUNK = 512
+M_TILES = CO // P
+BLOCK = 128
+MAX_LOAD = 4 * CHUNK
+RUN = 4
+SPIN_FIRST = 4
+SPIN_NEXT = 5
+EPS = 1e-5
+
+FLOPS = 2 * COLS * (CO * CV + CO * (CO + CH))
+
+
+def batch_parts(first, last):
+    parts = []
+    for b in range(BATCH):
+        lo = max(first, b * PIXELS)
+        hi = min(last, (b + 1) * PIXELS)
+        if lo < hi:
+            parts.append((b, lo - b * PIXELS, hi - b * PIXELS))
+    return parts
+
+
+def tile_afnb_pb_t_kernel(tc, context, high_feats, ww, bw, wf, bfuse, gf, bef, mf, vf, out):
+    nc = tc.nc
+    chunks = [(first, min(CHUNK, COLS - first)) for first in range(0, COLS, CHUNK)]
+    rounds = len(chunks)
+
+    ctx_rows = context.rearrange("b (p j) h w -> b p j (h w)", j=PACK)
+    hi_rows = high_feats.rearrange("b (p j) h w -> b p j (h w)", j=PACK)
+    out_rows = out.rearrange("b (p m) h w -> b p m (h w)", m=M_TILES)
+
+    with ExitStack() as stack:
+        keep = stack.enter_context(tc.tile_pool(name="keep", bufs=1))
+        work = stack.enter_context(tc.tile_pool(name="work", bufs=2))
+        psum = stack.enter_context(tc.psum_pool(name="psum", bufs=4))
+        stack.enter_context(tc.manual_schedule())
+
+        warm = keep.tile([P, 1], F32)
+        nc.vector.memset(warm[:], 1.0)
+        nc.scalar.sqrt(out=warm[:], in_=warm[:])
+
+        def load_vector(vec, name):
+            vec_sb = keep.tile([P, M_TILES], BF16, name=name)
+            nc.sync.dma_start(out=vec_sb[:], in_=vec.rearrange("(p m) -> p m", m=M_TILES))
+            return vec_sb
+
+        ww_sb = keep.tile([P, M_TILES * CV], BF16)
+        wf_sb = keep.tile([P, M_TILES * (CO + CH)], BF16)
+        nc.sync.dma_start(out=ww_sb[:], in_=ww.rearrange("(p m) k -> p (m k)", m=M_TILES))
+
+        load_starts = [0]
+        first, load_width = CHUNK, CHUNK
+        while first < COLS:
+            load_starts.append(first)
+            first += load_width
+            load_width = min(2 * load_width, MAX_LOAD)
+        ctx_raw, hi_raw = {}, {}
+        wanted = [(0, 1, "wf", 0, 0)]
+        for first, last in zip(load_starts, load_starts[1:] + [COLS]):
+            wanted.append((first // CHUNK - 2, 2, "ctx_raw", first, last))
+            wanted.append((first // CHUNK, 0, "hi_raw", first, last))
+        for need, rank, name, first, last in sorted(wanted):
+            if name == "wf":
+                nc.sync.dma_start(out=wf_sb[:], in_=wf.rearrange("(p m) k -> p (m k)", m=M_TILES))
+                gf_sb = load_vector(gf, "gf_sb")
+                bfuse_sb = load_vector(bfuse, "bfuse_sb")
+                mf_sb = load_vector(mf, "mf_sb")
+                bef_sb = load_vector(bef, "bef_sb")
+            else:
+                raw, rows = (ctx_raw, ctx_rows) if name == "ctx_raw" else (hi_raw, hi_rows)
+                raw[first] = keep.tile([P, PACK, last - first], BF16, name="%s_%d" % (name, first))
+                for b, n0, n1 in batch_parts(first, last):
+                    col = b * PIXELS + n0 - first
+                    nc.sync.dma_start(out=raw[first][:, :, col : col + n1 - n0], in_=rows[b, :, :, n0:n1])
+                if first == 0 and name == "ctx_raw":
+                    bw_sb = load_vector(bw, "bw_sb")
+                    vf_sb = load_vector(vf, "vf_sb")
+
+        ident = keep.tile([P, P], F32)
+        make_identity(nc, ident[:])
+
+        zeros = keep.tile([P, CHUNK], BF16)
+        nc.vector.memset(zeros[:], 0.0)
+
+        def spin(count):
+            idle = psum.tile([P, CHUNK], F32, name="idle", tag="c_acc")
+            for k in range(count):
+                nc.tensor.matmul(out=idle[:], lhsT=zeros[:, :P], rhs=zeros[:], start=True, stop=True)
+
+        spin(SPIN_FIRST)
+
+        def transpose_weight(w_sb, passes, name, copy_out):
+            words = w_sb[:].bitcast(F32).rearrange("p (m g q u) -> p m g u q", m=M_TILES, g=passes, u=2)
+            grouped = keep.tile([P, passes * M_TILES * P * PACK], BF16, align_bytes=64, name=name + "_grouped")
+            pairs = grouped[:].bitcast(F32).rearrange("q (g m c u) -> q g m c u", g=passes, m=M_TILES, u=2)
+            for g in range(passes):
+                for m0 in range(0, M_TILES, 2):
+                    bank = psum.tile([P, 2, 2, P], F32, name="w_bank", tag="y_acc")
+                    for i in range(2):
+                        for u in range(2):
+                            nc.tensor.transpose(bank[:, i, u, :], words[:, m0 + i, g, u, :], ident[:])
+                    copy_out(out=pairs[:, g, m0 : m0 + 2], in_=bank[:].rearrange("q i u c -> q i c u"))
+            return grouped
+
+        def weight_tiles(passes, name):
+            codes = keep.tile([P, passes, M_TILES, P], U32, align_bytes=64, name=name + "_codes")
+            scales = keep.tile([P, passes, M_TILES, P], U8, align_bytes=64, name=name + "_scales")
+            return codes, scales
+
+        def quantise_weight(grouped, codes, scales):
+            nc.vector.quantize_mx(
+                out=codes[:].rearrange("q g m c -> q (g m c)").bitcast(FP8X4),
+                scales=scales[:].rearrange("q g m c -> q (g m c)"),
+                in_=grouped[:],
+            )
+
+        grouped_of = {}
+        codes_of = {}
+        c_banks = {}
+
+        def raw_columns(raw, i, lo, hi):
+            first = chunks[i][0]
+            load = max(start for start in load_starts if start <= first)
+            return raw[load][:, :, first - load + lo : first - load + hi]
+
+        def by_runs(grouped, planes):
+            return (
+                grouped.rearrange("p (c i) t -> p c t i", i=RUN),
+                planes.rearrange("p t (c i) -> p c t i", i=RUN),
+            )
+
+        def regroup_ctx(i):
+            if not 0 <= i < rounds:
+                return
+            width = chunks[i][1]
+            grouped = work.tile([P, CHUNK, PACK], BF16, align_bytes=64, name="ctx_grouped", bufs=3)
+            split = width * 5 // 8 if i == 0 else width
+            dst, src = by_runs(grouped[:, :split, :], raw_columns(ctx_raw, i, 0, split))
+            nc.scalar.copy(out=dst, in_=src)
+            if split < width:
+                nc.gpsimd.tensor_scalar(
+                    out=grouped[:, split:width, :],
+                    in0=raw_columns(ctx_raw, i, split, width).rearrange("p t n -> p n t"),
+                    scalar1=1.0,
+                    scalar2=0.0,
+                    op0=MULT,
+                    op1=ADD,
+                )
+            grouped_of["ctx", i] = grouped
+
+        def regroup_hi_gpsimd(i):
+            if not 0 <= i < rounds:
+                return
+            width = chunks[i][1]
+            split = width * 3 // 4
+            grouped = work.tile([P, CHUNK, PACK], BF16, align_bytes=64, name="hi_grouped", bufs=1)
+            if i == 0:
+                nc.vector.memset(grouped[:, 0:1, :], 0.0)
+            nc.gpsimd.tensor_scalar(
+                out=grouped[:, :split, :],
+                in0=raw_columns(hi_raw, i, 0, split).rearrange("p t n -> p n t"),
+                scalar1=1.0,
+                scalar2=0.0,
+                op0=MULT,
+                op1=ADD,
+            )
+            grouped_of["hi", i] = grouped
+
+        def regroup_hi_vector(i):
+            if not 0 <= i < rounds:
+                return
+            width = chunks[i][1]
+            split = width * 3 // 4
+            dst, src = by_runs(grouped_of["hi", i][:, split:width, :], raw_columns(hi_raw, i, split, width))
+            nc.vector.tensor_copy(out=dst, in_=src)
+
+        def quantise_chunk(operand, i, bufs):
+            if not 0 <= i < rounds:
+                return
+            width = chunks[i][1]
+            codes = work.tile([P, CHUNK], U32, align_bytes=64, name=operand + "_codes", bufs=bufs)
+            scales = work.tile([P, CHUNK], U8, align_bytes=64, name=operand + "_scales", bufs=bufs)
+            nc.vector.quantize_mx(
+                out=codes[:, :width].bitcast(FP8X4),
+                scales=scales[:, :width],
+                in_=grouped_of[operand, i][:, :width, :].rearrange("p n t -> p (n t)"),
+            )
+            codes_of[operand, i] = (codes, scales)
+
+        def first_product(i):
+            if not 0 <= i < rounds:
+                return
+            width = chunks[i][1]
+            ctx_codes, ctx_scales = codes_of["ctx", i]
+            c_banks[i] = []
+            for n0 in range(0, width, BLOCK):
+                bank = psum.tile([P, M_TILES, BLOCK], F32, name="c_acc")
+                for m in range(M_TILES):
+                    nc.tensor.matmul_mx(
+                        out=bank[:, m, :],
+                        lhsT=ww_codes[:, 0, m, :].bitcast(FP8X4),
+                        lhsT_scale=ww_scales[:, 0, m, :],
+                        rhs=ctx_codes[:, n0 : n0 + BLOCK].bitcast(FP8X4),
+                        rhs_scale=ctx_scales[:, n0 : n0 + BLOCK],
+                        start=True,
+                        stop=True,
+                    )
+                c_banks[i].append(bank)
+
+        def drain_c(i):
+            if not 0 <= i < rounds:
+                return
+            grouped = work.tile([P, CHUNK, PACK], BF16, align_bytes=64, name="c_grouped")
+            for k, bank in enumerate(c_banks[i]):
+                nc.vector.tensor_tensor(
+                    out=grouped[:, k * BLOCK : (k + 1) * BLOCK, :],
+                    in0=bank[:].rearrange("p m n -> p n m"),
+                    in1=bw_f32[:].unsqueeze(1).to_broadcast([P, BLOCK, M_TILES]),
+                    op=ADD,
+                )
+            grouped_of["c", i] = grouped
+
+        def second_product(i):
+            if not 0 <= i < rounds:
+                return
+            first, width = chunks[i]
+            moving = [codes_of["c", i], codes_of["hi", i]]
+            vector_helps = i == rounds - 1
+            y_sb = work.tile([P, M_TILES, CHUNK], F32, bufs=6)
+            for m in range(M_TILES):
+                y_acc = psum.tile([P, CHUNK], F32)
+                for g in range(len(moving)):
+                    nc.tensor.matmul_mx(
+                        out=y_acc[:, :width],
+                        lhsT=wf_codes[:, g, m, :].bitcast(FP8X4),
+                        lhsT_scale=wf_scales[:, g, m, :],
+                        rhs=moving[g][0][:, :width].bitcast(FP8X4),
+                        rhs_scale=moving[g][1][:, :width],
+                        start=(g == 0),
+                        stop=(g == len(moving) - 1),
+                    )
+                if vector_helps and m % 2 == 1:
+                    nc.vector.tensor_scalar(
+                        out=y_sb[:, m, :width],
+                        in0=y_acc[:, :width],
+                        scalar1=bn_scale[:, m : m + 1],
+                        scalar2=bn_shift[:, m : m + 1],
+                        op0=MULT,
+                        op1=ADD,
+                    )
+                else:
+                    nc.scalar.activation(
+                        out=y_sb[:, m, :width],
+                        in_=y_acc[:, :width],
+                        func=IDENTITY,
+                        scale=bn_scale[:, m : m + 1],
+                        bias=bn_shift[:, m : m + 1],
+                    )
+                if i == rounds - 1:
+                    for b, n0, n1 in batch_parts(first, first + width):
+                        col = b * PIXELS + n0 - first
+                        nc.sync.dma_start(out=out_rows[b, :, m, n0:n1], in_=y_sb[:, m, col : col + n1 - n0])
+            if i < rounds - 1:
+                for b, n0, n1 in batch_parts(first, first + width):
+                    col = b * PIXELS + n0 - first
+                    nc.sync.dma_start(out=out_rows[b, :, :, n0:n1], in_=y_sb[:, :, col : col + n1 - n0])
+
+        bw_f32 = keep.tile([P, M_TILES], F32)
+        bn_scale = keep.tile([P, M_TILES], F32)
+        bn_shift = keep.tile([P, M_TILES], F32)
+
+        def prepare_second_product():
+            nc.vector.reciprocal(out=bn_scale[:], in_=bn_scale[:])
+            nc.vector.tensor_mul(out=bn_scale[:], in0=bn_scale[:], in1=gf_sb[:])
+            nc.vector.tensor_sub(out=bn_shift[:], in0=bfuse_sb[:], in1=mf_sb[:])
+            nc.vector.tensor_mul(out=bn_shift[:], in0=bn_shift[:], in1=bn_scale[:])
+            nc.vector.tensor_add(out=bn_shift[:], in0=bn_shift[:], in1=bef_sb[:])
+            quantise_weight(wf_grouped, wf_codes, wf_scales)
+
+        def one_round(i):
+            regroup_hi_gpsimd(i)
+            drain_c(i)
+            second_product(i - 1)
+            regroup_hi_vector(i)
+            quantise_chunk("ctx", i + 1, 2)
+            first_product(i + 1)
+            quantise_chunk("c", i, 2)
+            if i == 0:
+                prepare_second_product()
+            quantise_chunk("hi", i, 2)
+            regroup_ctx(i + 2)
+
+        ww_grouped = transpose_weight(ww_sb, CV // K_PASS, "ww", nc.vector.tensor_copy)
+        ww_codes, ww_scales = weight_tiles(CV // K_PASS, "ww")
+        wf_codes, wf_scales = weight_tiles((CO + CH) // K_PASS, "wf")
+        spin(SPIN_NEXT)
+        quantise_weight(ww_grouped, ww_codes, ww_scales)
+        regroup_ctx(0)
+        one_round(-1)
+        nc.vector.tensor_copy(out=bw_f32[:], in_=bw_sb[:])
+        nc.vector.tensor_scalar_add(out=bn_scale[:], in0=vf_sb[:], scalar1=EPS)
+        nc.scalar.sqrt(out=bn_scale[:], in_=bn_scale[:])
+        wf_grouped = transpose_weight(wf_sb, (CO + CH) // K_PASS, "wf", nc.scalar.copy)
+        for i in range(rounds + 1):
+            one_round(i)

@@ -173,13 +173,14 @@ def tile_afnb_pb_t_kernel(tc, context, high_feats, ww, bw, wf, bfuse, gf, bef, m
             if not 0 <= i < rounds:
                 return
             width = chunks[i][1]
-            split = width * 3 // 4
+            split = width * 7 // 8
             grouped = work.tile([P, CHUNK, PACK], BF16, align_bytes=64, name="hi_grouped", bufs=1)
             if i == 0:
                 nc.vector.memset(grouped[:, 0:1, :], 0.0)
+            dst, src = by_runs(grouped[:, :split, :], raw_columns(hi_raw, i, 0, split))
             nc.gpsimd.tensor_scalar(
-                out=grouped[:, :split, :],
-                in0=raw_columns(hi_raw, i, 0, split).rearrange("p t n -> p n t"),
+                out=dst,
+                in0=src,
                 scalar1=1.0,
                 scalar2=0.0,
                 op0=MULT,
@@ -191,7 +192,7 @@ def tile_afnb_pb_t_kernel(tc, context, high_feats, ww, bw, wf, bfuse, gf, bef, m
             if not 0 <= i < rounds:
                 return
             width = chunks[i][1]
-            split = width * 3 // 4
+            split = width * 7 // 8
             dst, src = by_runs(grouped_of["hi", i][:, split:width, :], raw_columns(hi_raw, i, split, width))
             nc.vector.tensor_copy(out=dst, in_=src)
 

@@ -66,7 +66,7 @@ def tile_afnb_pb_t_kernel(tc, context, high_feats, ww, bw, wf, bfuse, gf, bef, m
             return vec_sb
 
         ww_sb = keep.tile([P, M_TILES * CV], BF16)
-        wf_sb = keep.tile([P, M_TILES * (CO + CH)], BF16)
+        wf_sb = [keep.tile([P, M_TILES * K_PASS], BF16, name="wf_sb_%d" % g) for g in range((CO + CH) // K_PASS)]
         nc.sync.dma_start(out=ww_sb[:], in_=ww.rearrange("(p m) k -> p (m k)", m=M_TILES))
 
         load_starts = [0]
@@ -82,7 +82,11 @@ def tile_afnb_pb_t_kernel(tc, context, high_feats, ww, bw, wf, bfuse, gf, bef, m
             wanted.append((first // CHUNK, 0, "hi_raw", first, last))
         for need, rank, name, first, last in sorted(wanted):
             if name == "wf":
-                nc.sync.dma_start(out=wf_sb[:], in_=wf.rearrange("(p m) k -> p (m k)", m=M_TILES))
+                for g, part in enumerate(wf_sb):
+                    nc.sync.dma_start(
+                        out=part[:].rearrange("p (m k) -> p m k", m=M_TILES),
+                        in_=wf.rearrange("(p m) (g k) -> g p m k", m=M_TILES, g=len(wf_sb))[g],
+                    )
                 gf_sb = load_vector(gf, "gf_sb")
                 bfuse_sb = load_vector(bfuse, "bfuse_sb")
                 mf_sb = load_vector(mf, "mf_sb")
@@ -110,16 +114,17 @@ def tile_afnb_pb_t_kernel(tc, context, high_feats, ww, bw, wf, bfuse, gf, bef, m
 
         spin(SPIN_FIRST)
 
-        def transpose_weight(w_sb, passes, name, copy_out):
-            words = w_sb[:].bitcast(F32).rearrange("p (m g q u) -> p m g u q", m=M_TILES, g=passes, u=2)
+        def transpose_weight(parts, name, copy_out):
+            passes = len(parts)
             grouped = keep.tile([P, passes * M_TILES * P * PACK], BF16, align_bytes=64, name=name + "_grouped")
             pairs = grouped[:].bitcast(F32).rearrange("q (g m c u) -> q g m c u", g=passes, m=M_TILES, u=2)
-            for g in range(passes):
+            for g, part in enumerate(parts):
+                words = part[:].bitcast(F32).rearrange("p (m q u) -> p m u q", m=M_TILES, u=2)
                 for m0 in range(0, M_TILES, 2):
                     bank = psum.tile([P, 2, 2, P], F32, name="w_bank", tag="y_acc")
                     for i in range(2):
                         for u in range(2):
-                            nc.tensor.transpose(bank[:, i, u, :], words[:, m0 + i, g, u, :], ident[:])
+                            nc.tensor.transpose(bank[:, i, u, :], words[:, m0 + i, u, :], ident[:])
                     copy_out(out=pairs[:, g, m0 : m0 + 2], in_=bank[:].rearrange("q i u c -> q i c u"))
             return grouped
 
@@ -278,11 +283,11 @@ def tile_afnb_pb_t_kernel(tc, context, high_feats, ww, bw, wf, bfuse, gf, bef, m
                         scale=bn_scale[:, m : m + 1],
                         bias=bn_shift[:, m : m + 1],
                     )
-                if i == rounds - 1:
+                if i >= rounds - 2:
                     for b, n0, n1 in batch_parts(first, first + width):
                         col = b * PIXELS + n0 - first
                         nc.sync.dma_start(out=out_rows[b, :, m, n0:n1], in_=y_sb[:, m, col : col + n1 - n0])
-            if i < rounds - 1:
+            if i < rounds - 2:
                 for b, n0, n1 in batch_parts(first, first + width):
                     col = b * PIXELS + n0 - first
                     nc.sync.dma_start(out=out_rows[b, :, :, n0:n1], in_=y_sb[:, :, col : col + n1 - n0])
@@ -291,28 +296,37 @@ def tile_afnb_pb_t_kernel(tc, context, high_feats, ww, bw, wf, bfuse, gf, bef, m
         bn_scale = keep.tile([P, M_TILES], F32)
         bn_shift = keep.tile([P, M_TILES], F32)
 
-        def prepare_second_product():
-            nc.vector.reciprocal(out=bn_scale[:], in_=bn_scale[:])
-            nc.vector.tensor_mul(out=bn_scale[:], in0=bn_scale[:], in1=gf_sb[:])
-            nc.vector.tensor_sub(out=bn_shift[:], in0=bfuse_sb[:], in1=mf_sb[:])
-            nc.vector.tensor_mul(out=bn_shift[:], in0=bn_shift[:], in1=bn_scale[:])
-            nc.vector.tensor_add(out=bn_shift[:], in0=bn_shift[:], in1=bef_sb[:])
-            quantise_weight(wf_grouped, wf_codes, wf_scales)
+        batch_norm_steps = [
+            lambda: nc.vector.reciprocal(out=bn_scale[:], in_=bn_scale[:]),
+            lambda: nc.vector.tensor_mul(out=bn_scale[:], in0=bn_scale[:], in1=gf_sb[:]),
+            lambda: nc.vector.tensor_sub(out=bn_shift[:], in0=bfuse_sb[:], in1=mf_sb[:]),
+            lambda: nc.vector.tensor_mul(out=bn_shift[:], in0=bn_shift[:], in1=bn_scale[:]),
+            lambda: nc.vector.tensor_add(out=bn_shift[:], in0=bn_shift[:], in1=bef_sb[:]),
+        ]
+
+        def batch_norm_step(i, *steps):
+            if i == 0:
+                for step in steps:
+                    batch_norm_steps[step]()
 
         def one_round(i):
             regroup_hi_gpsimd(i)
             drain_c(i)
             second_product(i - 1)
+            batch_norm_step(i, 0, 2)
             regroup_hi_vector(i)
+            batch_norm_step(i, 1)
             quantise_chunk("ctx", i + 1, 2)
             first_product(i + 1)
+            batch_norm_step(i, 3)
             quantise_chunk("c", i, 2)
+            batch_norm_step(i, 4)
             if i == 0:
-                prepare_second_product()
+                quantise_weight(wf_grouped, wf_codes, wf_scales)
             quantise_chunk("hi", i, 2)
             regroup_ctx(i + 2)
 
-        ww_grouped = transpose_weight(ww_sb, CV // K_PASS, "ww", nc.vector.tensor_copy)
+        ww_grouped = transpose_weight([ww_sb], "ww", nc.vector.tensor_copy)
         ww_codes, ww_scales = weight_tiles(CV // K_PASS, "ww")
         wf_codes, wf_scales = weight_tiles((CO + CH) // K_PASS, "wf")
         spin(SPIN_NEXT)
@@ -322,6 +336,6 @@ def tile_afnb_pb_t_kernel(tc, context, high_feats, ww, bw, wf, bfuse, gf, bef, m
         nc.vector.tensor_copy(out=bw_f32[:], in_=bw_sb[:])
         nc.vector.tensor_scalar_add(out=bn_scale[:], in0=vf_sb[:], scalar1=EPS)
         nc.scalar.sqrt(out=bn_scale[:], in_=bn_scale[:])
-        wf_grouped = transpose_weight(wf_sb, (CO + CH) // K_PASS, "wf", nc.scalar.copy)
+        wf_grouped = transpose_weight(wf_sb, "wf", nc.scalar.copy)
         for i in range(rounds + 1):
             one_round(i)

@@ -24,8 +24,8 @@ M_TILES = CO // P
 BLOCK = 128
 MAX_LOAD = 4 * CHUNK
 RUN = 4
-SPIN_FIRST = 4
-SPIN_NEXT = 5
+SPIN_FIRST = 8
+SPIN_NEXT = 4
 EPS = 1e-5
 
 FLOPS = 2 * COLS * (CO * CV + CO * (CO + CH))
@@ -67,21 +67,27 @@ def tile_afnb_pb_t_kernel(tc, context, high_feats, ww, bw, wf, bfuse, gf, bef, m
 
         ww_sb = keep.tile([P, M_TILES * CV], BF16)
         wf_sb = [keep.tile([P, M_TILES * K_PASS], BF16, name="wf_sb_%d" % g) for g in range((CO + CH) // K_PASS)]
-        nc.sync.dma_start(out=ww_sb[:], in_=ww.rearrange("(p m) k -> p (m k)", m=M_TILES))
 
         load_starts = [0]
-        first, load_width = CHUNK, CHUNK
+        load_starts += [CHUNK * i for i in range(1, 4)]
+        first, load_width = CHUNK * 4, 2 * CHUNK
         while first < COLS:
             load_starts.append(first)
             first += load_width
             load_width = min(2 * load_width, MAX_LOAD)
         ctx_raw, hi_raw = {}, {}
-        wanted = [(0, 1, "wf", 0, 0)]
+        wanted = [(0, 1, "wf", 0, 0), (-2, 3, "ww", 0, 0)]
         for first, last in zip(load_starts, load_starts[1:] + [COLS]):
             wanted.append((first // CHUNK - 2, 2, "ctx_raw", first, last))
             wanted.append((first // CHUNK, 0, "hi_raw", first, last))
         for need, rank, name, first, last in sorted(wanted):
-            if name == "wf":
+            if name == "ww":
+                for half in range(2):
+                    nc.sync.dma_start(
+                        out=ww_sb[:].rearrange("p (h r) -> p h r", h=2)[:, half, :],
+                        in_=ww.rearrange("(p h m) k -> h p (m k)", h=2, m=M_TILES // 2)[half],
+                    )
+            elif name == "wf":
                 for g, part in enumerate(wf_sb):
                     nc.sync.dma_start(
                         out=part[:].rearrange("p (m k) -> p m k", m=M_TILES),
@@ -133,12 +139,16 @@ def tile_afnb_pb_t_kernel(tc, context, high_feats, ww, bw, wf, bfuse, gf, bef, m
             scales = keep.tile([P, passes, M_TILES, P], U8, align_bytes=64, name=name + "_scales")
             return codes, scales
 
-        def quantise_weight(grouped, codes, scales):
-            nc.vector.quantize_mx(
-                out=codes[:].rearrange("q g m c -> q (g m c)").bitcast(FP8X4),
-                scales=scales[:].rearrange("q g m c -> q (g m c)"),
-                in_=grouped[:],
-            )
+        def quantise_weight(grouped, codes, scales, calls):
+            words = codes[:].rearrange("q g m c -> q (g m c)")
+            scale_bytes = scales[:].rearrange("q g m c -> q (g m c)")
+            step = words.shape[1] // calls
+            for lo in range(0, calls * step, step):
+                nc.vector.quantize_mx(
+                    out=words[:, lo : lo + step].bitcast(FP8X4),
+                    scales=scale_bytes[:, lo : lo + step],
+                    in_=grouped[:, lo * PACK : (lo + step) * PACK],
+                )
 
         grouped_of = {}
         codes_of = {}
@@ -160,25 +170,19 @@ def tile_afnb_pb_t_kernel(tc, context, high_feats, ww, bw, wf, bfuse, gf, bef, m
                 return
             width = chunks[i][1]
             grouped = work.tile([P, CHUNK, PACK], BF16, align_bytes=64, name="ctx_grouped", bufs=3)
-            split = width * 5 // 8 if i == 0 else width
+            split = width // 2 if i == 0 else width
             dst, src = by_runs(grouped[:, :split, :], raw_columns(ctx_raw, i, 0, split))
             nc.scalar.copy(out=dst, in_=src)
             if split < width:
-                nc.gpsimd.tensor_scalar(
-                    out=grouped[:, split:width, :],
-                    in0=raw_columns(ctx_raw, i, split, width).rearrange("p t n -> p n t"),
-                    scalar1=1.0,
-                    scalar2=0.0,
-                    op0=MULT,
-                    op1=ADD,
-                )
+                dst, src = by_runs(grouped[:, split:width, :], raw_columns(ctx_raw, i, split, width))
+                nc.vector.tensor_copy(out=dst, in_=src)
             grouped_of["ctx", i] = grouped
 
         def regroup_hi_gpsimd(i):
             if not 0 <= i < rounds:
                 return
             width = chunks[i][1]
-            split = width * 7 // 8
+            split = width * 27 // 32
             grouped = work.tile([P, CHUNK, PACK], BF16, align_bytes=64, name="hi_grouped", bufs=1)
             if i == 0:
                 nc.vector.memset(grouped[:, 0:1, :], 0.0)
@@ -197,7 +201,7 @@ def tile_afnb_pb_t_kernel(tc, context, high_feats, ww, bw, wf, bfuse, gf, bef, m
             if not 0 <= i < rounds:
                 return
             width = chunks[i][1]
-            split = width * 7 // 8
+            split = width * 27 // 32
             dst, src = by_runs(grouped_of["hi", i][:, split:width, :], raw_columns(hi_raw, i, split, width))
             nc.vector.tensor_copy(out=dst, in_=src)
 
@@ -283,11 +287,11 @@ def tile_afnb_pb_t_kernel(tc, context, high_feats, ww, bw, wf, bfuse, gf, bef, m
                         scale=bn_scale[:, m : m + 1],
                         bias=bn_shift[:, m : m + 1],
                     )
-                if i >= rounds - 2:
+                if i >= rounds - 3:
                     for b, n0, n1 in batch_parts(first, first + width):
                         col = b * PIXELS + n0 - first
                         nc.sync.dma_start(out=out_rows[b, :, m, n0:n1], in_=y_sb[:, m, col : col + n1 - n0])
-            if i < rounds - 2:
+            if i < rounds - 3:
                 for b, n0, n1 in batch_parts(first, first + width):
                     col = b * PIXELS + n0 - first
                     nc.sync.dma_start(out=out_rows[b, :, :, n0:n1], in_=y_sb[:, :, col : col + n1 - n0])
@@ -322,19 +326,21 @@ def tile_afnb_pb_t_kernel(tc, context, high_feats, ww, bw, wf, bfuse, gf, bef, m
             quantise_chunk("c", i, 2)
             batch_norm_step(i, 4)
             if i == 0:
-                quantise_weight(wf_grouped, wf_codes, wf_scales)
+                quantise_weight(wf_grouped, wf_codes, wf_scales, 1)
             quantise_chunk("hi", i, 2)
             regroup_ctx(i + 2)
 
-        ww_grouped = transpose_weight([ww_sb], "ww", nc.vector.tensor_copy)
+        regroup_ctx(0)
+        nc.vector.tensor_copy(out=bw_f32[:], in_=bw_sb[:])
+        nc.vector.tensor_scalar_add(out=bn_scale[:], in0=vf_sb[:], scalar1=EPS)
+        ww_grouped = transpose_weight([ww_sb], "ww", nc.scalar.copy)
         ww_codes, ww_scales = weight_tiles(CV // K_PASS, "ww")
         wf_codes, wf_scales = weight_tiles((CO + CH) // K_PASS, "wf")
         spin(SPIN_NEXT)
-        quantise_weight(ww_grouped, ww_codes, ww_scales)
-        regroup_ctx(0)
-        one_round(-1)
-        nc.vector.tensor_copy(out=bw_f32[:], in_=bw_sb[:])
-        nc.vector.tensor_scalar_add(out=bn_scale[:], in0=vf_sb[:], scalar1=EPS)
+        quantise_chunk("ctx", 0, 2)
+        quantise_weight(ww_grouped, ww_codes, ww_scales, 2)
+        first_product(0)
+        regroup_ctx(1)
         nc.scalar.sqrt(out=bn_scale[:], in_=bn_scale[:])
         wf_grouped = transpose_weight(wf_sb, "wf", nc.scalar.copy)
         for i in range(rounds + 1):

@@ -24,8 +24,8 @@ M_TILES = CO // P
 BLOCK = 128
 MAX_LOAD = 4 * CHUNK
 RUN = 4
-SPIN_FIRST = 8
-SPIN_NEXT = 4
+SPIN_FIRST = 5
+SPIN_NEXT = 2
 EPS = 1e-5
 
 FLOPS = 2 * COLS * (CO * CV + CO * (CO + CH))
@@ -69,8 +69,7 @@ def tile_afnb_pb_t_kernel(tc, context, high_feats, ww, bw, wf, bfuse, gf, bef, m
         wf_sb = [keep.tile([P, M_TILES * K_PASS], BF16, name="wf_sb_%d" % g) for g in range((CO + CH) // K_PASS)]
 
         load_starts = [0]
-        load_starts += [CHUNK * i for i in range(1, 4)]
-        first, load_width = CHUNK * 4, 2 * CHUNK
+        first, load_width = CHUNK, CHUNK
         while first < COLS:
             load_starts.append(first)
             first += load_width
@@ -103,7 +102,7 @@ def tile_afnb_pb_t_kernel(tc, context, high_feats, ww, bw, wf, bfuse, gf, bef, m
                 for b, n0, n1 in batch_parts(first, last):
                     col = b * PIXELS + n0 - first
                     nc.sync.dma_start(out=raw[first][:, :, col : col + n1 - n0], in_=rows[b, :, :, n0:n1])
-                if first == 0 and name == "ctx_raw":
+                if first == CHUNK and name == "ctx_raw":
                     bw_sb = load_vector(bw, "bw_sb")
                     vf_sb = load_vector(vf, "vf_sb")
 
@@ -182,7 +181,7 @@ def tile_afnb_pb_t_kernel(tc, context, high_feats, ww, bw, wf, bfuse, gf, bef, m
             if not 0 <= i < rounds:
                 return
             width = chunks[i][1]
-            split = width * 27 // 32
+            split = width * 7 // 8
             grouped = work.tile([P, CHUNK, PACK], BF16, align_bytes=64, name="hi_grouped", bufs=1)
             if i == 0:
                 nc.vector.memset(grouped[:, 0:1, :], 0.0)
@@ -201,7 +200,7 @@ def tile_afnb_pb_t_kernel(tc, context, high_feats, ww, bw, wf, bfuse, gf, bef, m
             if not 0 <= i < rounds:
                 return
             width = chunks[i][1]
-            split = width * 27 // 32
+            split = width * 7 // 8
             dst, src = by_runs(grouped_of["hi", i][:, split:width, :], raw_columns(hi_raw, i, split, width))
             nc.vector.tensor_copy(out=dst, in_=src)
 
@@ -331,8 +330,6 @@ def tile_afnb_pb_t_kernel(tc, context, high_feats, ww, bw, wf, bfuse, gf, bef, m
             regroup_ctx(i + 2)
 
         regroup_ctx(0)
-        nc.vector.tensor_copy(out=bw_f32[:], in_=bw_sb[:])
-        nc.vector.tensor_scalar_add(out=bn_scale[:], in0=vf_sb[:], scalar1=EPS)
         ww_grouped = transpose_weight([ww_sb], "ww", nc.scalar.copy)
         ww_codes, ww_scales = weight_tiles(CV // K_PASS, "ww")
         wf_codes, wf_scales = weight_tiles((CO + CH) // K_PASS, "wf")
@@ -340,6 +337,8 @@ def tile_afnb_pb_t_kernel(tc, context, high_feats, ww, bw, wf, bfuse, gf, bef, m
         quantise_chunk("ctx", 0, 2)
         quantise_weight(ww_grouped, ww_codes, ww_scales, 2)
         first_product(0)
+        nc.vector.tensor_copy(out=bw_f32[:], in_=bw_sb[:])
+        nc.vector.tensor_scalar_add(out=bn_scale[:], in0=vf_sb[:], scalar1=EPS)
         regroup_ctx(1)
         nc.scalar.sqrt(out=bn_scale[:], in_=bn_scale[:])
         wf_grouped = transpose_weight(wf_sb, "wf", nc.scalar.copy)

@@ -22,10 +22,11 @@ COLS = BATCH * PIXELS
 CHUNK = 512
 M_TILES = CO // P
 BLOCK = 128
-MAX_LOAD = 4 * CHUNK
 RUN = 4
 SPIN_FIRST = 5
 SPIN_NEXT = 2
+PAIRED = 10
+Y_TILES = 4
 EPS = 1e-5
 
 FLOPS = 2 * COLS * (CO * CV + CO * (CO + CH))
@@ -66,36 +67,35 @@ def tile_afnb_pb_t_kernel(tc, context, high_feats, ww, bw, wf, bfuse, gf, bef, m
             return vec_sb
 
         ww_sb = keep.tile([P, M_TILES * CV], BF16)
-        wf_sb = [keep.tile([P, M_TILES * K_PASS], BF16, name="wf_sb_%d" % g) for g in range((CO + CH) // K_PASS)]
+        ww_halves = [ww_sb[:, half * 2 * CV : (half + 1) * 2 * CV] for half in range(2)]
+        wf_size = M_TILES * (CO + CH)
+        wf_stage = work.tile([P, 2 * wf_size], BF16, align_bytes=64, name="y_sb", bufs=Y_TILES)
+        wf_halves = [wf_stage[:, half * wf_size // 2 : (half + 1) * wf_size // 2] for half in range(2)]
+        wf_grouped = wf_stage[:, wf_size : 2 * wf_size]
+        ww_grouped = keep.tile([P, M_TILES * CV], BF16, align_bytes=64)
 
-        load_starts = [0]
-        first, load_width = CHUNK, CHUNK
-        while first < COLS:
-            load_starts.append(first)
-            first += load_width
-            load_width = min(2 * load_width, MAX_LOAD)
+        def load_weight(halves, weight):
+            for half, part in enumerate(halves):
+                nc.sync.dma_start(out=part, in_=weight.rearrange("(p h m) k -> h p (m k)", h=2, m=M_TILES // 2)[half])
+
+
+        ctx_starts = [chunk * CHUNK for chunk in (0, 1, 2, 3, 5, 8)]
+        hi_starts = [chunk * CHUNK for chunk in (0, 1, 2, 4, 8)]
         ctx_raw, hi_raw = {}, {}
         wanted = [(0, 1, "wf", 0, 0), (-2, 3, "ww", 0, 0)]
-        for first, last in zip(load_starts, load_starts[1:] + [COLS]):
+        for first, last in zip(ctx_starts, ctx_starts[1:] + [COLS]):
             wanted.append((first // CHUNK - 2, 2, "ctx_raw", first, last))
+        for first, last in zip(hi_starts, hi_starts[1:] + [COLS]):
             wanted.append((first // CHUNK, 0, "hi_raw", first, last))
         for need, rank, name, first, last in sorted(wanted):
             if name == "ww":
-                for half in range(2):
-                    nc.sync.dma_start(
-                        out=ww_sb[:].rearrange("p (h r) -> p h r", h=2)[:, half, :],
-                        in_=ww.rearrange("(p h m) k -> h p (m k)", h=2, m=M_TILES // 2)[half],
-                    )
+                load_weight(ww_halves, ww)
             elif name == "wf":
-                for g, part in enumerate(wf_sb):
-                    nc.sync.dma_start(
-                        out=part[:].rearrange("p (m k) -> p m k", m=M_TILES),
-                        in_=wf.rearrange("(p m) (g k) -> g p m k", m=M_TILES, g=len(wf_sb))[g],
-                    )
                 gf_sb = load_vector(gf, "gf_sb")
                 bfuse_sb = load_vector(bfuse, "bfuse_sb")
                 mf_sb = load_vector(mf, "mf_sb")
                 bef_sb = load_vector(bef, "bef_sb")
+                load_weight(wf_halves, wf)
             else:
                 raw, rows = (ctx_raw, ctx_rows) if name == "ctx_raw" else (hi_raw, hi_rows)
                 raw[first] = keep.tile([P, PACK, last - first], BF16, name="%s_%d" % (name, first))
@@ -119,43 +119,43 @@ def tile_afnb_pb_t_kernel(tc, context, high_feats, ww, bw, wf, bfuse, gf, bef, m
 
         spin(SPIN_FIRST)
 
-        def transpose_weight(parts, name, copy_out):
-            passes = len(parts)
-            grouped = keep.tile([P, passes * M_TILES * P * PACK], BF16, align_bytes=64, name=name + "_grouped")
-            pairs = grouped[:].bitcast(F32).rearrange("q (g m c u) -> q g m c u", g=passes, m=M_TILES, u=2)
-            for g, part in enumerate(parts):
-                words = part[:].bitcast(F32).rearrange("p (m q u) -> p m u q", m=M_TILES, u=2)
-                for m0 in range(0, M_TILES, 2):
+        def transpose_weight(halves, passes):
+            banks = {}
+            for h, half in enumerate(halves):
+                words = half.bitcast(F32).rearrange("p (i g q u) -> p i g u q", i=2, g=passes, u=2)
+                for g in range(passes):
                     bank = psum.tile([P, 2, 2, P], F32, name="w_bank", tag="y_acc")
                     for i in range(2):
                         for u in range(2):
-                            nc.tensor.transpose(bank[:, i, u, :], words[:, m0 + i, u, :], ident[:])
-                    copy_out(out=pairs[:, g, m0 : m0 + 2], in_=bank[:].rearrange("q i u c -> q i c u"))
-            return grouped
+                            nc.tensor.transpose(bank[:, i, u, :], words[:, i, g, u, :], ident[:])
+                    banks[h, g] = bank
+            return banks
+
+        def copy_weight(copy, banks, passes, grouped, h, g):
+            pairs = grouped.bitcast(F32).rearrange("q (g m c u) -> q g m c u", g=passes, m=M_TILES, u=2)
+            copy(out=pairs[:, g, 2 * h : 2 * h + 2], in_=banks[h, g][:].rearrange("q i u c -> q i c u"))
 
         def weight_tiles(passes, name):
             codes = keep.tile([P, passes, M_TILES, P], U32, align_bytes=64, name=name + "_codes")
             scales = keep.tile([P, passes, M_TILES, P], U8, align_bytes=64, name=name + "_scales")
             return codes, scales
 
-        def quantise_weight(grouped, codes, scales, calls):
-            words = codes[:].rearrange("q g m c -> q (g m c)")
-            scale_bytes = scales[:].rearrange("q g m c -> q (g m c)")
-            step = words.shape[1] // calls
-            for lo in range(0, calls * step, step):
-                nc.vector.quantize_mx(
-                    out=words[:, lo : lo + step].bitcast(FP8X4),
-                    scales=scale_bytes[:, lo : lo + step],
-                    in_=grouped[:, lo * PACK : (lo + step) * PACK],
-                )
+        def quantise_weight(grouped, codes, scales, g, h):
+            lo = (g * M_TILES + 2 * h) * P
+            nc.vector.quantize_mx(
+                out=codes[:].rearrange("q g m c -> q (g m c)")[:, lo : lo + 2 * P].bitcast(FP8X4),
+                scales=scales[:].rearrange("q g m c -> q (g m c)")[:, lo : lo + 2 * P],
+                in_=grouped[:, lo * PACK : (lo + 2 * P) * PACK],
+            )
 
         grouped_of = {}
         codes_of = {}
+        y_tiles = {}
         c_banks = {}
 
         def raw_columns(raw, i, lo, hi):
             first = chunks[i][0]
-            load = max(start for start in load_starts if start <= first)
+            load = max(start for start in raw if start <= first)
             return raw[load][:, :, first - load + lo : first - load + hi]
 
         def by_runs(grouped, planes):
@@ -177,11 +177,15 @@ def tile_afnb_pb_t_kernel(tc, context, high_feats, ww, bw, wf, bfuse, gf, bef, m
                 nc.vector.tensor_copy(out=dst, in_=src)
             grouped_of["ctx", i] = grouped
 
+        def hi_shares(i):
+            width = chunks[i][1]
+            return (width // 2 if i == 0 else width * 7 // 8, width * 7 // 8)
+
         def regroup_hi_gpsimd(i):
             if not 0 <= i < rounds:
                 return
             width = chunks[i][1]
-            split = width * 7 // 8
+            split, vector_start = hi_shares(i)
             grouped = work.tile([P, CHUNK, PACK], BF16, align_bytes=64, name="hi_grouped", bufs=1)
             if i == 0:
                 nc.vector.memset(grouped[:, 0:1, :], 0.0)
@@ -194,13 +198,16 @@ def tile_afnb_pb_t_kernel(tc, context, high_feats, ww, bw, wf, bfuse, gf, bef, m
                 op0=MULT,
                 op1=ADD,
             )
+            if split < vector_start:
+                dst, src = by_runs(grouped[:, split:vector_start, :], raw_columns(hi_raw, i, split, vector_start))
+                nc.scalar.copy(out=dst, in_=src)
             grouped_of["hi", i] = grouped
 
         def regroup_hi_vector(i):
             if not 0 <= i < rounds:
                 return
             width = chunks[i][1]
-            split = width * 7 // 8
+            split = hi_shares(i)[1]
             dst, src = by_runs(grouped_of["hi", i][:, split:width, :], raw_columns(hi_raw, i, split, width))
             nc.vector.tensor_copy(out=dst, in_=src)
 
@@ -256,7 +263,13 @@ def tile_afnb_pb_t_kernel(tc, context, high_feats, ww, bw, wf, bfuse, gf, bef, m
             first, width = chunks[i]
             moving = [codes_of["c", i], codes_of["hi", i]]
             vector_helps = i == rounds - 1
-            y_sb = work.tile([P, M_TILES, CHUNK], F32, bufs=6)
+            paired = i < PAIRED
+            if not paired or i % 2 == 0:
+                y_tiles[i] = work.tile([P, M_TILES, 2 * CHUNK], F32, align_bytes=64, name="y_sb", bufs=Y_TILES)
+            else:
+                y_tiles[i] = y_tiles[i - 1]
+            at = CHUNK if paired and i % 2 == 1 else 0
+            y_sb = y_tiles[i][:, :, at : at + CHUNK]
             for m in range(M_TILES):
                 y_acc = psum.tile([P, CHUNK], F32)
                 for g in range(len(moving)):
@@ -290,10 +303,11 @@ def tile_afnb_pb_t_kernel(tc, context, high_feats, ww, bw, wf, bfuse, gf, bef, m
                     for b, n0, n1 in batch_parts(first, first + width):
                         col = b * PIXELS + n0 - first
                         nc.sync.dma_start(out=out_rows[b, :, m, n0:n1], in_=y_sb[:, m, col : col + n1 - n0])
-            if i < rounds - 3:
-                for b, n0, n1 in batch_parts(first, first + width):
-                    col = b * PIXELS + n0 - first
-                    nc.sync.dma_start(out=out_rows[b, :, :, n0:n1], in_=y_sb[:, :, col : col + n1 - n0])
+            if i < rounds - 3 and not (paired and i % 2 == 0):
+                start = first - at
+                for b, n0, n1 in batch_parts(start, first + width):
+                    col = b * PIXELS + n0 - start
+                    nc.sync.dma_start(out=out_rows[b, :, :, n0:n1], in_=y_tiles[i][:, :, col : col + n1 - n0])
 
         bw_f32 = keep.tile([P, M_TILES], F32)
         bn_scale = keep.tile([P, M_TILES], F32)
@@ -313,7 +327,8 @@ def tile_afnb_pb_t_kernel(tc, context, high_feats, ww, bw, wf, bfuse, gf, bef, m
                     batch_norm_steps[step]()
 
         def one_round(i):
-            regroup_hi_gpsimd(i)
+            if i > 0:
+                regroup_hi_gpsimd(i)
             drain_c(i)
             second_product(i - 1)
             batch_norm_step(i, 0, 2)
@@ -325,22 +340,32 @@ def tile_afnb_pb_t_kernel(tc, context, high_feats, ww, bw, wf, bfuse, gf, bef, m
             quantise_chunk("c", i, 2)
             batch_norm_step(i, 4)
             if i == 0:
-                quantise_weight(wf_grouped, wf_codes, wf_scales, 1)
+                quantise_weight(wf_grouped, wf_codes, wf_scales, 0, 0)
+                quantise_weight(wf_grouped, wf_codes, wf_scales, 1, 0)
+                copy_weight(nc.vector.tensor_copy, wf_banks, 2, wf_grouped, 1, 1)
+                quantise_weight(wf_grouped, wf_codes, wf_scales, 0, 1)
+                quantise_weight(wf_grouped, wf_codes, wf_scales, 1, 1)
             quantise_chunk("hi", i, 2)
             regroup_ctx(i + 2)
 
         regroup_ctx(0)
-        ww_grouped = transpose_weight([ww_sb], "ww", nc.scalar.copy)
+        ww_banks = transpose_weight(ww_halves, 1)
+        for h in range(2):
+            copy_weight(nc.scalar.copy, ww_banks, 1, ww_grouped[:], h, 0)
         ww_codes, ww_scales = weight_tiles(CV // K_PASS, "ww")
         wf_codes, wf_scales = weight_tiles((CO + CH) // K_PASS, "wf")
         spin(SPIN_NEXT)
         quantise_chunk("ctx", 0, 2)
-        quantise_weight(ww_grouped, ww_codes, ww_scales, 2)
+        for h in range(2):
+            quantise_weight(ww_grouped, ww_codes, ww_scales, 0, h)
         first_product(0)
         nc.vector.tensor_copy(out=bw_f32[:], in_=bw_sb[:])
         nc.vector.tensor_scalar_add(out=bn_scale[:], in0=vf_sb[:], scalar1=EPS)
         regroup_ctx(1)
         nc.scalar.sqrt(out=bn_scale[:], in_=bn_scale[:])
-        wf_grouped = transpose_weight(wf_sb, "wf", nc.scalar.copy)
+        regroup_hi_gpsimd(0)
+        wf_banks = transpose_weight(wf_halves, 2)
+        for h, g in [(0, 0), (0, 1), (1, 0)]:
+            copy_weight(nc.scalar.copy, wf_banks, 2, wf_grouped, h, g)
         for i in range(rounds + 1):
             one_round(i)

@@ -80,7 +80,7 @@ def tile_afnb_pb_t_kernel(tc, context, high_feats, ww, bw, wf, bfuse, gf, bef, m
 
 
         ctx_starts = [chunk * CHUNK for chunk in (0, 1, 2, 3, 5, 8)]
-        hi_starts = [chunk * CHUNK for chunk in (0, 1, 2, 4, 8)]
+        hi_starts = [chunk * CHUNK for chunk in (0, 1, 2, 3, 5, 8)]
         ctx_raw, hi_raw = {}, {}
         wanted = [(0, 1, "wf", 0, 0), (-2, 3, "ww", 0, 0)]
         for first, last in zip(ctx_starts, ctx_starts[1:] + [COLS]):
@@ -91,11 +91,11 @@ def tile_afnb_pb_t_kernel(tc, context, high_feats, ww, bw, wf, bfuse, gf, bef, m
             if name == "ww":
                 load_weight(ww_halves, ww)
             elif name == "wf":
+                load_weight(wf_halves, wf)
                 gf_sb = load_vector(gf, "gf_sb")
                 bfuse_sb = load_vector(bfuse, "bfuse_sb")
                 mf_sb = load_vector(mf, "mf_sb")
                 bef_sb = load_vector(bef, "bef_sb")
-                load_weight(wf_halves, wf)
             else:
                 raw, rows = (ctx_raw, ctx_rows) if name == "ctx_raw" else (hi_raw, hi_rows)
                 raw[first] = keep.tile([P, PACK, last - first], BF16, name="%s_%d" % (name, first))
@@ -179,7 +179,7 @@ def tile_afnb_pb_t_kernel(tc, context, high_feats, ww, bw, wf, bfuse, gf, bef, m
 
         def hi_shares(i):
             width = chunks[i][1]
-            return (width // 2 if i == 0 else width * 7 // 8, width * 7 // 8)
+            return (width // 2 if i == 0 else width * 13 // 16, width * 13 // 16)
 
         def regroup_hi_gpsimd(i):
             if not 0 <= i < rounds:
@@ -331,19 +331,19 @@ def tile_afnb_pb_t_kernel(tc, context, high_feats, ww, bw, wf, bfuse, gf, bef, m
                 regroup_hi_gpsimd(i)
             drain_c(i)
             second_product(i - 1)
-            batch_norm_step(i, 0, 2)
             regroup_hi_vector(i)
-            batch_norm_step(i, 1)
+            batch_norm_step(i, 0)
             quantise_chunk("ctx", i + 1, 2)
             first_product(i + 1)
-            batch_norm_step(i, 3)
             quantise_chunk("c", i, 2)
-            batch_norm_step(i, 4)
             if i == 0:
                 quantise_weight(wf_grouped, wf_codes, wf_scales, 0, 0)
+                batch_norm_step(i, 1, 2)
                 quantise_weight(wf_grouped, wf_codes, wf_scales, 1, 0)
                 copy_weight(nc.vector.tensor_copy, wf_banks, 2, wf_grouped, 1, 1)
+                batch_norm_step(i, 3)
                 quantise_weight(wf_grouped, wf_codes, wf_scales, 0, 1)
+                batch_norm_step(i, 4)
                 quantise_weight(wf_grouped, wf_codes, wf_scales, 1, 1)
             quantise_chunk("hi", i, 2)
             regroup_ctx(i + 2)

from contextlib import ExitStack

import concourse.mybir as mybir
from concourse.masks import make_identity

F32 = mybir.dt.float32
BF16 = mybir.dt.bfloat16
U32 = mybir.dt.uint32
U8 = mybir.dt.uint8
FP8X4 = mybir.dt.float8_e4m3fn_x4
IDENTITY = mybir.ActivationFunctionType.Identity
MULT = mybir.AluOpType.mult
ADD = mybir.AluOpType.add

P = 128
PACK = 4
K_PASS = P * PACK

BATCH, PIXELS = 2, 48 * 72
CV, CH, CO = 512, 512, 512
COLS = BATCH * PIXELS
CHUNK = 512
M_TILES = CO // P
BLOCK = 128
RUN = 4
SPIN_FIRST = 5
SPIN_NEXT = 2
PAIRED = 10
Y_TILES = 4
EPS = 1e-5

FLOPS = 2 * COLS * (CO * CV + CO * (CO + CH))


def batch_parts(first, last):
    parts = []
    for b in range(BATCH):
        lo = max(first, b * PIXELS)
        hi = min(last, (b + 1) * PIXELS)
        if lo < hi:
            parts.append((b, lo - b * PIXELS, hi - b * PIXELS))
    return parts


def tile_afnb_pb_t_kernel(tc, context, high_feats, ww, bw, wf, bfuse, gf, bef, mf, vf, out):
    nc = tc.nc
    chunks = [(first, min(CHUNK, COLS - first)) for first in range(0, COLS, CHUNK)]
    rounds = len(chunks)

    ctx_rows = context.rearrange("b (p j) h w -> b p j (h w)", j=PACK)
    hi_rows = high_feats.rearrange("b (p j) h w -> b p j (h w)", j=PACK)
    out_rows = out.rearrange("b (p m) h w -> b p m (h w)", m=M_TILES)

    with ExitStack() as stack:
        keep = stack.enter_context(tc.tile_pool(name="keep", bufs=1))
        work = stack.enter_context(tc.tile_pool(name="work", bufs=2))
        psum = stack.enter_context(tc.psum_pool(name="psum", bufs=4))
        stack.enter_context(tc.manual_schedule())

        warm = keep.tile([P, 1], F32)
        nc.vector.memset(warm[:], 1.0)
        nc.scalar.sqrt(out=warm[:], in_=warm[:])

        def load_vector(vec, name):
            vec_sb = keep.tile([P, M_TILES], BF16, name=name)
            nc.sync.dma_start(out=vec_sb[:], in_=vec.rearrange("(p m) -> p m", m=M_TILES))
            return vec_sb

        ww_sb = keep.tile([P, M_TILES * CV], BF16)
        ww_halves = [ww_sb[:, half * 2 * CV : (half + 1) * 2 * CV] for half in range(2)]
        wf_size = M_TILES * (CO + CH)
        wf_stage = work.tile([P, 2 * wf_size], BF16, align_bytes=64, name="y_sb", bufs=Y_TILES)
        wf_halves = [wf_stage[:, half * wf_size // 2 : (half + 1) * wf_size // 2] for half in range(2)]
        wf_grouped = wf_stage[:, wf_size : 2 * wf_size]
        ww_grouped = keep.tile([P, M_TILES * CV], BF16, align_bytes=64)

        def load_weight(halves, weight):
            for half, part in enumerate(halves):
                nc.sync.dma_start(out=part, in_=weight.rearrange("(p h m) k -> h p (m k)", h=2, m=M_TILES // 2)[half])


        ctx_starts = [chunk * CHUNK for chunk in (0, 1, 2, 3, 5, 8)]
        hi_starts = [chunk * CHUNK for chunk in (0, 1, 2, 3, 5, 8)]
        ctx_raw, hi_raw = {}, {}
        wanted = [(0, 1, "wf", 0, 0), (-2, 3, "ww", 0, 0)]
        for first, last in zip(ctx_starts, ctx_starts[1:] + [COLS]):
            wanted.append((first // CHUNK - 2, 2, "ctx_raw", first, last))
        for first, last in zip(hi_starts, hi_starts[1:] + [COLS]):
            wanted.append((first // CHUNK, 0, "hi_raw", first, last))
        for need, rank, name, first, last in sorted(wanted):
            if name == "ww":
                load_weight(ww_halves, ww)
            elif name == "wf":
                load_weight(wf_halves, wf)
                gf_sb = load_vector(gf, "gf_sb")
                bfuse_sb = load_vector(bfuse, "bfuse_sb")
                mf_sb = load_vector(mf, "mf_sb")
                bef_sb = load_vector(bef, "bef_sb")
            else:
                raw, rows = (ctx_raw, ctx_rows) if name == "ctx_raw" else (hi_raw, hi_rows)
                raw[first] = keep.tile([P, PACK, last - first], BF16, name="%s_%d" % (name, first))
                for b, n0, n1 in batch_parts(first, last):
                    col = b * PIXELS + n0 - first
                    nc.sync.dma_start(out=raw[first][:, :, col : col + n1 - n0], in_=rows[b, :, :, n0:n1])
                if first == CHUNK and name == "ctx_raw":
                    bw_sb = load_vector(bw, "bw_sb")
                    vf_sb = load_vector(vf, "vf_sb")

        ident = keep.tile([P, P], F32)
        make_identity(nc, ident[:])

        zeros = keep.tile([P, CHUNK], BF16)
        nc.vector.memset(zeros[:], 0.0)

        def spin(count):
            idle = psum.tile([P, CHUNK], F32, name="idle", tag="c_acc")
            for k in range(count):
                nc.tensor.matmul(out=idle[:], lhsT=zeros[:, :P], rhs=zeros[:], start=True, stop=True)

        spin(SPIN_FIRST)

        def transpose_weight(halves, passes):
            banks = {}
            for h, half in enumerate(halves):
                words = half.bitcast(F32).rearrange("p (i g q u) -> p i g u q", i=2, g=passes, u=2)
                for g in range(passes):
                    bank = psum.tile([P, 2, 2, P], F32, name="w_bank", tag="y_acc")
                    for i in range(2):
                        for u in range(2):
                            nc.tensor.transpose(bank[:, i, u, :], words[:, i, g, u, :], ident[:])
                    banks[h, g] = bank
            return banks

        def copy_weight(copy, banks, passes, grouped, h, g):
            pairs = grouped.bitcast(F32).rearrange("q (g m c u) -> q g m c u", g=passes, m=M_TILES, u=2)
            copy(out=pairs[:, g, 2 * h : 2 * h + 2], in_=banks[h, g][:].rearrange("q i u c -> q i c u"))

        def weight_tiles(passes, name):
            codes = keep.tile([P, passes, M_TILES, P], U32, align_bytes=64, name=name + "_codes")
            scales = keep.tile([P, passes, M_TILES, P], U8, align_bytes=64, name=name + "_scales")
            return codes, scales

        def quantise_weight(grouped, codes, scales, g, h):
            lo = (g * M_TILES + 2 * h) * P
            nc.vector.quantize_mx(
                out=codes[:].rearrange("q g m c -> q (g m c)")[:, lo : lo + 2 * P].bitcast(FP8X4),
                scales=scales[:].rearrange("q g m c -> q (g m c)")[:, lo : lo + 2 * P],
                in_=grouped[:, lo * PACK : (lo + 2 * P) * PACK],
            )

        grouped_of = {}
        codes_of = {}
        y_tiles = {}
        c_banks = {}

        def raw_columns(raw, i, lo, hi):
            first = chunks[i][0]
            load = max(start for start in raw if start <= first)
            return raw[load][:, :, first - load + lo : first - load + hi]

        def by_runs(grouped, planes):
            return (
                grouped.rearrange("p (c i) t -> p c t i", i=RUN),
                planes.rearrange("p t (c i) -> p c t i", i=RUN),
            )

        def regroup_ctx(i):
            if not 0 <= i < rounds:
                return
            width = chunks[i][1]
            grouped = work.tile([P, CHUNK, PACK], BF16, align_bytes=64, name="ctx_grouped", bufs=3)
            split = width // 2 if i == 0 else width
            dst, src = by_runs(grouped[:, :split, :], raw_columns(ctx_raw, i, 0, split))
            nc.scalar.copy(out=dst, in_=src)
            if split < width:
                dst, src = by_runs(grouped[:, split:width, :], raw_columns(ctx_raw, i, split, width))
                nc.vector.tensor_copy(out=dst, in_=src)
            grouped_of["ctx", i] = grouped

        def hi_shares(i):
            width = chunks[i][1]
            return (width // 2 if i == 0 else width * 13 // 16, width * 13 // 16)

        def regroup_hi_gpsimd(i):
            if not 0 <= i < rounds:
                return
            width = chunks[i][1]
            split, vector_start = hi_shares(i)
            grouped = work.tile([P, CHUNK, PACK], BF16, align_bytes=64, name="hi_grouped", bufs=1)
            if i == 0:
                nc.vector.memset(grouped[:, 0:1, :], 0.0)
            dst, src = by_runs(grouped[:, :split, :], raw_columns(hi_raw, i, 0, split))
            nc.gpsimd.tensor_scalar(
                out=dst,
                in0=src,
                scalar1=1.0,
                scalar2=0.0,
                op0=MULT,
                op1=ADD,
            )
            if split < vector_start:
                dst, src = by_runs(grouped[:, split:vector_start, :], raw_columns(hi_raw, i, split, vector_start))
                nc.scalar.copy(out=dst, in_=src)
            grouped_of["hi", i] = grouped

        def regroup_hi_vector(i):
            if not 0 <= i < rounds:
                return
            width = chunks[i][1]
            split = hi_shares(i)[1]
            dst, src = by_runs(grouped_of["hi", i][:, split:width, :], raw_columns(hi_raw, i, split, width))
            nc.vector.tensor_copy(out=dst, in_=src)

        def quantise_chunk(operand, i, bufs):
            if not 0 <= i < rounds:
                return
            width = chunks[i][1]
            codes = work.tile([P, CHUNK], U32, align_bytes=64, name=operand + "_codes", bufs=bufs)
            scales = work.tile([P, CHUNK], U8, align_bytes=64, name=operand + "_scales", bufs=bufs)
            nc.vector.quantize_mx(
                out=codes[:, :width].bitcast(FP8X4),
                scales=scales[:, :width],
                in_=grouped_of[operand, i][:, :width, :].rearrange("p n t -> p (n t)"),
            )
            codes_of[operand, i] = (codes, scales)

        def first_product(i):
            if not 0 <= i < rounds:
                return
            width = chunks[i][1]
            ctx_codes, ctx_scales = codes_of["ctx", i]
            c_banks[i] = []
            for n0 in range(0, width, BLOCK):
                bank = psum.tile([P, M_TILES, BLOCK], F32, name="c_acc")
                for m in range(M_TILES):
                    nc.tensor.matmul_mx(
                        out=bank[:, m, :],
                        lhsT=ww_codes[:, 0, m, :].bitcast(FP8X4),
                        lhsT_scale=ww_scales[:, 0, m, :],
                        rhs=ctx_codes[:, n0 : n0 + BLOCK].bitcast(FP8X4),
                        rhs_scale=ctx_scales[:, n0 : n0 + BLOCK],
                        start=True,
                        stop=True,
                    )
                c_banks[i].append(bank)

        def drain_c(i):
            if not 0 <= i < rounds:
                return
            grouped = work.tile([P, CHUNK, PACK], BF16, align_bytes=64, name="c_grouped")
            for k, bank in enumerate(c_banks[i]):
                nc.vector.tensor_tensor(
                    out=grouped[:, k * BLOCK : (k + 1) * BLOCK, :],
                    in0=bank[:].rearrange("p m n -> p n m"),
                    in1=bw_f32[:].unsqueeze(1).to_broadcast([P, BLOCK, M_TILES]),
                    op=ADD,
                )
            grouped_of["c", i] = grouped

        def second_product(i):
            if not 0 <= i < rounds:
                return
            first, width = chunks[i]
            moving = [codes_of["c", i], codes_of["hi", i]]
            vector_helps = i == rounds - 1
            paired = i < PAIRED
            if not paired or i % 2 == 0:
                y_tiles[i] = work.tile([P, M_TILES, 2 * CHUNK], F32, align_bytes=64, name="y_sb", bufs=Y_TILES)
            else:
                y_tiles[i] = y_tiles[i - 1]
            at = CHUNK if paired and i % 2 == 1 else 0
            y_sb = y_tiles[i][:, :, at : at + CHUNK]
            for m in range(M_TILES):
                y_acc = psum.tile([P, CHUNK], F32)
                for g in range(len(moving)):
                    nc.tensor.matmul_mx(
                        out=y_acc[:, :width],
                        lhsT=wf_codes[:, g, m, :].bitcast(FP8X4),
                        lhsT_scale=wf_scales[:, g, m, :],
                        rhs=moving[g][0][:, :width].bitcast(FP8X4),
                        rhs_scale=moving[g][1][:, :width],
                        start=(g == 0),
                        stop=(g == len(moving) - 1),
                    )
                if vector_helps and m % 2 == 1:
                    nc.vector.tensor_scalar(
                        out=y_sb[:, m, :width],
                        in0=y_acc[:, :width],
                        scalar1=bn_scale[:, m : m + 1],
                        scalar2=bn_shift[:, m : m + 1],
                        op0=MULT,
                        op1=ADD,
                    )
                else:
                    nc.scalar.activation(
                        out=y_sb[:, m, :width],
                        in_=y_acc[:, :width],
                        func=IDENTITY,
                        scale=bn_scale[:, m : m + 1],
                        bias=bn_shift[:, m : m + 1],
                    )
                if i >= rounds - 3:
                    for b, n0, n1 in batch_parts(first, first + width):
                        col = b * PIXELS + n0 - first
                        nc.sync.dma_start(out=out_rows[b, :, m, n0:n1], in_=y_sb[:, m, col : col + n1 - n0])
            if i < rounds - 3 and not (paired and i % 2 == 0):
                start = first - at
                for b, n0, n1 in batch_parts(start, first + width):
                    col = b * PIXELS + n0 - start
                    nc.sync.dma_start(out=out_rows[b, :, :, n0:n1], in_=y_tiles[i][:, :, col : col + n1 - n0])

        bw_f32 = keep.tile([P, M_TILES], F32)
        bn_scale = keep.tile([P, M_TILES], F32)
        bn_shift = keep.tile([P, M_TILES], F32)

        batch_norm_steps = [
            lambda: nc.vector.reciprocal(out=bn_scale[:], in_=bn_scale[:]),
            lambda: nc.vector.tensor_mul(out=bn_scale[:], in0=bn_scale[:], in1=gf_sb[:]),
            lambda: nc.vector.tensor_sub(out=bn_shift[:], in0=bfuse_sb[:], in1=mf_sb[:]),
            lambda: nc.vector.tensor_mul(out=bn_shift[:], in0=bn_shift[:], in1=bn_scale[:]),
            lambda: nc.vector.tensor_add(out=bn_shift[:], in0=bn_shift[:], in1=bef_sb[:]),
        ]

        def batch_norm_step(i, *steps):
            if i == 0:
                for step in steps:
                    batch_norm_steps[step]()

        def one_round(i):
            if i > 0:
                regroup_hi_gpsimd(i)
            drain_c(i)
            second_product(i - 1)
            regroup_hi_vector(i)
            batch_norm_step(i, 0)
            quantise_chunk("ctx", i + 1, 2)
            first_product(i + 1)
            quantise_chunk("c", i, 2)
            if i == 0:
                quantise_weight(wf_grouped, wf_codes, wf_scales, 0, 0)
                batch_norm_step(i, 1, 2)
                quantise_weight(wf_grouped, wf_codes, wf_scales, 1, 0)
                copy_weight(nc.vector.tensor_copy, wf_banks, 2, wf_grouped, 1, 1)
                batch_norm_step(i, 3)
                quantise_weight(wf_grouped, wf_codes, wf_scales, 0, 1)
                batch_norm_step(i, 4)
                quantise_weight(wf_grouped, wf_codes, wf_scales, 1, 1)
            quantise_chunk("hi", i, 2)
            regroup_ctx(i + 2)

        regroup_ctx(0)
        ww_banks = transpose_weight(ww_halves, 1)
        for h in range(2):
            copy_weight(nc.scalar.copy, ww_banks, 1, ww_grouped[:], h, 0)
        ww_codes, ww_scales = weight_tiles(CV // K_PASS, "ww")
        wf_codes, wf_scales = weight_tiles((CO + CH) // K_PASS, "wf")
        spin(SPIN_NEXT)
        quantise_chunk("ctx", 0, 2)
        for h in range(2):
            quantise_weight(ww_grouped, ww_codes, ww_scales, 0, h)
        first_product(0)
        nc.vector.tensor_copy(out=bw_f32[:], in_=bw_sb[:])
        nc.vector.tensor_scalar_add(out=bn_scale[:], in0=vf_sb[:], scalar1=EPS)
        regroup_ctx(1)
        nc.scalar.sqrt(out=bn_scale[:], in_=bn_scale[:])
        regroup_hi_gpsimd(0)
        wf_banks = transpose_weight(wf_halves, 2)
        for h, g in [(0, 0), (0, 1), (1, 0)]:
            copy_weight(nc.scalar.copy, wf_banks, 2, wf_grouped, h, g)
        for i in range(rounds + 1):
            one_round(i)
